import numpy as np
import ml_dtypes


def mxq(x, axis, fmt="e4m3"):
    dtype, down = {"e4m3": (ml_dtypes.float8_e4m3fn, 7), "e5m2": (ml_dtypes.float8_e5m2, 14)}[fmt]
    v = np.moveaxis(np.asarray(x, np.float32).astype(ml_dtypes.bfloat16).astype(np.float64), axis, -1)
    blocks = v.reshape(v.shape[:-1] + (-1, 32))
    amax = np.abs(blocks).max(-1, keepdims=True)
    byte = np.maximum(np.where(amax > 0, np.frexp(amax)[1] - 1 + 127, 0) - down, 1)
    scale = np.exp2(byte - 127.0)
    codes = (blocks / scale).astype(np.float32).astype(dtype).astype(np.float64)
    return np.moveaxis((codes * scale).reshape(v.shape), -1, axis)


WIDE = False


def mx_kscale(k):
    if not WIDE:
        return np.ones(k)
    levels = np.array([10, -10, 5, -5, 0])
    if k % 512:
        return np.exp2(np.random.permutation(np.resize(levels, k // 32))).repeat(32)
    a = np.empty((k // 512, 16))
    for p in range(k // 512):
        a[p, :8] = np.random.permutation(np.resize(levels, 8))
        for g in range(8):
            far = levels[np.abs(levels - a[p, g]) >= 10]
            a[p, g + 8] = far[np.random.randint(len(far))]
    return np.exp2(a.ravel()).repeat(32)


BF16 = ml_dtypes.bfloat16


def bf(x):
    return np.asarray(x, np.float32).astype(BF16)


def f64(x):
    return np.asarray(x).astype(np.float64)


B, S, HID, NH, DH = 4, 2048, 256, 16, 64
DQ = NH * DH


def setup_inputs():
    s = mx_kscale(DQ)
    y = np.random.standard_normal((B, S, DQ)) * 0.3 * s
    h = np.ascontiguousarray(y.reshape(B, NH, S, DH).transpose(0, 2, 1, 3))
    return {"h_attn": bf(h),
            "Wo": bf(np.random.standard_normal((DQ, HID)) * 1.5 / np.sqrt(DQ) / s[:, None]),
            "bo": bf(np.random.standard_normal(HID) * 0.3)}


def reference(h_attn, Wo, bo):
    y = f64(h_attn).transpose(0, 2, 1, 3).reshape(B, -1, DQ)
    return (mxq(y, 2, "e4m3") @ mxq(f64(Wo), 0, "e4m3")) + f64(bo)

@@ -1,0 +1,174 @@
+from contextlib import ExitStack
+
+import concourse.mybir as mybir
+from concourse.masks import make_identity
+
+BF16 = mybir.dt.bfloat16
+F32 = mybir.dt.float32
+U32 = mybir.dt.uint32
+U8 = mybir.dt.uint8
+FP8X4 = mybir.dt.float8_e4m3fn_x4
+
+P = 128
+BATCH = 4
+TOKENS = 2048
+HEADS = 16
+DH = 64
+HID = 256
+TOKENS_PER_ROW = 16
+PASSES = 2
+J_PER_PASS = TOKENS_PER_ROW // PASSES
+PLANES = 2
+WORDS = DH // 2
+QUAD = 4
+QUADS = HEADS // QUAD
+PER_BANK = 2
+BANKS = QUAD // PER_BANK
+BLOCKS_PER_BATCH = PASSES * QUADS
+N_BLOCKS = BATCH * BLOCKS_PER_BATCH
+N_PRODUCTS = BATCH * QUADS
+
+FLOPS = 2 * BATCH * TOKENS * (TOKENS_PER_ROW * DH) * HID
+
+
+def tile_reasoningmultiheadattention_pb_t_kernel(tc, h_attn, Wo, bo, out):
+    nc = tc.nc
+    with ExitStack() as ctx:
+        const = ctx.enter_context(tc.tile_pool(name="const", bufs=1))
+        x_pool = ctx.enter_context(tc.tile_pool(name="x", bufs=BATCH * PASSES))
+        heads_pool = ctx.enter_context(tc.tile_pool(name="heads", bufs=3))
+        grouped_pool = ctx.enter_context(tc.tile_pool(name="grouped", bufs=3))
+        codes_pool = ctx.enter_context(tc.tile_pool(name="codes", bufs=2 * QUADS + 2))
+        res_pool = ctx.enter_context(tc.tile_pool(name="res", bufs=18))
+        psum_t = ctx.enter_context(tc.psum_pool(name="psum_t", bufs=4))
+        psum_o = ctx.enter_context(tc.psum_pool(name="psum_o", bufs=4))
+        ctx.enter_context(tc.manual_schedule())
+
+        w_raw = const.tile([P, PASSES, 2 * PLANES, HID], BF16)
+        nc.sync.dma_start(
+            out=w_raw[:].rearrange("p g t n -> p g (t n)"),
+            in_=Wo.rearrange("(g p t) n -> p g (t n)", p=P, t=2 * PLANES),
+        )
+        bias_row = const.tile([P, HID], BF16)
+        nc.vector.memset(bias_row[:], 0.0)
+        nc.sync.dma_start(out=bias_row[0:1, :], in_=bo.rearrange("(o n) -> o n", o=1))
+        x_half = {}
+        for b in range(BATCH):
+            halves = h_attn[b].rearrange("(r g j) h d -> g r j h d", g=PASSES, j=J_PER_PASS)
+            for g in range(PASSES):
+                x = x_pool.tile([P, J_PER_PASS, HEADS, DH], BF16)
+                nc.sync.dma_start(out=x[:], in_=halves[g])
+                x_half[(b, g)] = x
+
+        ident = const.tile([P, P], F32)
+        make_identity(nc, ident[:])
+        ones = const.tile([P, P], BF16)
+        nc.vector.memset(ones[:], 1.0)
+
+        w_grouped = const.tile([P, PASSES, HID, 2 * PLANES], BF16, align_bytes=64)
+        nc.vector.tensor_copy(out=w_grouped[:], in_=w_raw[:].rearrange("p g t n -> p g n t"))
+        w_codes = const.tile([P, PASSES * HID], U32, align_bytes=64)
+        w_scales = const.tile([P, PASSES * HID], U8, align_bytes=64)
+        nc.vector.quantize_mx(
+            out=w_codes[:].bitcast(FP8X4),
+            scales=w_scales[:],
+            in_=w_grouped[:].rearrange("p g n t -> p (g n t)"),
+        )
+
+        bias_ps = psum_o.tile([P, PER_BANK, HID], F32, tag="acc")
+        for c in range(PER_BANK):
+            nc.tensor.matmul(
+                out=bias_ps[:, c, :], lhsT=ones[:], rhs=bias_row[:], start=True, stop=True
+            )
+        bias = const.tile([P, PER_BANK, HID], F32)
+        nc.scalar.copy(out=bias[:], in_=bias_ps[:])
+
+        def where(block):
+            return block // BLOCKS_PER_BATCH, (block // QUADS) % PASSES, block % QUADS
+
+        heads_of, banks_of, grouped_of, codes_of, scales_of, acc_of = {}, {}, {}, {}, {}, {}
+
+        def regroup(block):
+            b, g, quad = where(block)
+            x = x_half[(b, g)]
+            mine = slice(quad * QUAD, (quad + 1) * QUAD)
+            heads = heads_pool.tile([P, QUAD, PLANES, J_PER_PASS, WORDS // PLANES], F32)
+            words = x[:].bitcast(F32)[:, :, mine, :].rearrange("p j h (w u) -> p h u j w", u=PLANES)
+            if b > 0 and (block % BLOCKS_PER_BATCH) % 3 == 1:
+                nc.scalar.copy(out=heads[:], in_=words)
+            else:
+                nc.vector.tensor_copy(out=heads[:], in_=words)
+            heads_of[block] = heads
+
+        def transpose(block):
+            words = heads_of[block][:].rearrange("p h u j w -> p h u (j w)")
+            banks_of[block] = []
+            for half in range(BANKS):
+                bank = psum_t.tile([P, PLANES, PER_BANK * P], F32)
+                for h in range(PER_BANK):
+                    for u in range(PLANES):
+                        nc.tensor.transpose(
+                            bank[:, u, h * P : (h + 1) * P], words[:, half * PER_BANK + h, u, :], ident[:]
+                        )
+                banks_of[block].append(bank)
+
+        def interleave(block):
+            grouped = grouped_pool.tile([P, QUAD, P, 2 * PLANES], BF16, align_bytes=64)
+            words = grouped[:].bitcast(F32)
+            for half, bank in enumerate(banks_of[block]):
+                nc.scalar.copy(
+                    out=words[:, half * PER_BANK : (half + 1) * PER_BANK, :, :],
+                    in_=bank[:].rearrange("p u (m c) -> p c m u", c=PER_BANK),
+                )
+            grouped_of[block] = grouped
+
+        def quantise(block):
+            codes = codes_pool.tile([P, QUAD * P], U32, align_bytes=64)
+            scales = codes_pool.tile([P, QUAD * P], U8, align_bytes=64)
+            nc.vector.quantize_mx(
+                out=codes[:].bitcast(FP8X4),
+                scales=scales[:],
+                in_=grouped_of[block][:].rearrange("p c m t -> p (c m t)"),
+            )
+            codes_of[block], scales_of[block] = codes, scales
+
+        def multiply(product):
+            b, quad = product // QUADS, product % QUADS
+            block_of_pass = [b * BLOCKS_PER_BATCH + g * QUADS + quad for g in range(PASSES)]
+            acc_of[product] = []
+            for half in range(BANKS):
+                acc = psum_o.tile([P, PER_BANK, HID], F32, tag="acc")
+                for c in range(PER_BANK):
+                    row_tile = slice((half * PER_BANK + c) * P, (half * PER_BANK + c + 1) * P)
+                    for g in range(PASSES):
+                        n_cols = slice(g * HID, (g + 1) * HID)
+                        nc.tensor.matmul_mx(
+                            out=acc[:, c, :],
+                            lhsT=codes_of[block_of_pass[g]][:, row_tile].bitcast(FP8X4),
+                            lhsT_scale=scales_of[block_of_pass[g]][:, row_tile],
+                            rhs=w_codes[:, n_cols].bitcast(FP8X4),
+                            rhs_scale=w_scales[:, n_cols],
+                            start=(g == 0),
+                            stop=(g == PASSES - 1),
+                        )
+                acc_of[product].append(acc)
+
+        def add_bias_and_store(product):
+            b, quad = product // QUADS, product % QUADS
+            slabs = out[b].rearrange("(s m c) n -> s m c n", m=P, c=PER_BANK)
+            for half, acc in enumerate(acc_of[product]):
+                res = res_pool.tile([P, PER_BANK, HID], F32)
+                nc.vector.tensor_tensor(out=res[:], in0=acc[:], in1=bias[:], op=mybir.AluOpType.add)
+                nc.sync.dma_start(out=slabs[quad * BANKS + half], in_=res[:])
+
+        block_stages = [regroup, transpose, interleave, quantise]
+        first_multiply = QUADS + len(block_stages)
+        steps_per_product = N_BLOCKS // N_PRODUCTS
+        for step in range(first_multiply + steps_per_product * (N_PRODUCTS - 1) + 2):
+            for lag, stage in enumerate(block_stages):
+                if 0 <= step - lag < N_BLOCKS:
+                    stage(step - lag)
+            for lag, stage in enumerate([multiply, add_bias_and_store], start=first_multiply):
+                if step >= lag and (step - lag) % steps_per_product == 0:
+                    if (step - lag) // steps_per_product < N_PRODUCTS:
+                        stage((step - lag) // steps_per_product)

@@ -39,7 +39,7 @@ def tile_reasoningmultiheadattention_pb_t_kernel(tc, h_attn, Wo, bo, out):
         heads_pool = ctx.enter_context(tc.tile_pool(name="heads", bufs=3))
         grouped_pool = ctx.enter_context(tc.tile_pool(name="grouped", bufs=3))
         codes_pool = ctx.enter_context(tc.tile_pool(name="codes", bufs=2 * QUADS + 2))
-        res_pool = ctx.enter_context(tc.tile_pool(name="res", bufs=18))
+        res_pool = ctx.enter_context(tc.tile_pool(name="res", bufs=9))
         psum_t = ctx.enter_context(tc.psum_pool(name="psum_t", bufs=4))
         psum_o = ctx.enter_context(tc.psum_pool(name="psum_o", bufs=4))
         ctx.enter_context(tc.manual_schedule())
@@ -117,8 +117,8 @@ def tile_reasoningmultiheadattention_pb_t_kernel(tc, h_attn, Wo, bo, out):
             words = grouped[:].bitcast(F32)
             for half, bank in enumerate(banks_of[block]):
                 nc.scalar.copy(
-                    out=words[:, half * PER_BANK : (half + 1) * PER_BANK, :, :],
-                    in_=bank[:].rearrange("p u (m c) -> p c m u", c=PER_BANK),
+                    out=words[:, :, half * P // BANKS : (half + 1) * P // BANKS, :],
+                    in_=bank[:].rearrange("p u (m c) -> p c m u", c=QUAD),
                 )
             grouped_of[block] = grouped
 
@@ -155,11 +155,16 @@ def tile_reasoningmultiheadattention_pb_t_kernel(tc, h_attn, Wo, bo, out):
 
         def add_bias_and_store(product):
             b, quad = product // QUADS, product % QUADS
-            slabs = out[b].rearrange("(s m c) n -> s m c n", m=P, c=PER_BANK)
+            slabs = out[b].rearrange("(s m c) n -> s m c n", m=P, c=QUAD)
+            res = res_pool.tile([P, QUAD, HID], F32)
             for half, acc in enumerate(acc_of[product]):
-                res = res_pool.tile([P, PER_BANK, HID], F32)
-                nc.vector.tensor_tensor(out=res[:], in0=acc[:], in1=bias[:], op=mybir.AluOpType.add)
-                nc.sync.dma_start(out=slabs[quad * BANKS + half], in_=res[:])
+                nc.vector.tensor_tensor(
+                    out=res[:, half * PER_BANK : (half + 1) * PER_BANK, :],
+                    in0=acc[:],
+                    in1=bias[:],
+                    op=mybir.AluOpType.add,
+                )
+            nc.sync.dma_start(out=slabs[quad], in_=res[:])
 
         block_stages = [regroup, transpose, interleave, quantise]
         first_multiply = QUADS + len(block_stages)

@@ -35,11 +35,11 @@ def tile_reasoningmultiheadattention_pb_t_kernel(tc, h_attn, Wo, bo, out):
     nc = tc.nc
     with ExitStack() as ctx:
         const = ctx.enter_context(tc.tile_pool(name="const", bufs=1))
-        x_pool = ctx.enter_context(tc.tile_pool(name="x", bufs=BATCH * PASSES))
-        heads_pool = ctx.enter_context(tc.tile_pool(name="heads", bufs=3))
-        grouped_pool = ctx.enter_context(tc.tile_pool(name="grouped", bufs=3))
-        codes_pool = ctx.enter_context(tc.tile_pool(name="codes", bufs=2 * QUADS + 2))
-        res_pool = ctx.enter_context(tc.tile_pool(name="res", bufs=9))
+        x_pool = ctx.enter_context(tc.tile_pool(name="x", bufs=6))
+        heads_pool = ctx.enter_context(tc.tile_pool(name="heads", bufs=5))
+        grouped_pool = ctx.enter_context(tc.tile_pool(name="grouped", bufs=5))
+        codes_pool = ctx.enter_context(tc.tile_pool(name="codes", bufs=2 * QUADS + 1))
+        res_pool = ctx.enter_context(tc.tile_pool(name="res", bufs=14))
         psum_t = ctx.enter_context(tc.psum_pool(name="psum_t", bufs=4))
         psum_o = ctx.enter_context(tc.psum_pool(name="psum_o", bufs=4))
         ctx.enter_context(tc.manual_schedule())
@@ -53,12 +53,15 @@ def tile_reasoningmultiheadattention_pb_t_kernel(tc, h_attn, Wo, bo, out):
         nc.vector.memset(bias_row[:], 0.0)
         nc.sync.dma_start(out=bias_row[0:1, :], in_=bo.rearrange("(o n) -> o n", o=1))
         x_half = {}
-        for b in range(BATCH):
+
+        def load(b):
             halves = h_attn[b].rearrange("(r g j) h d -> g r j h d", g=PASSES, j=J_PER_PASS)
             for g in range(PASSES):
-                x = x_pool.tile([P, J_PER_PASS, HEADS, DH], BF16)
-                nc.sync.dma_start(out=x[:], in_=halves[g])
-                x_half[(b, g)] = x
+                x_half[(b, g)] = x_pool.tile([P, J_PER_PASS, HEADS, DH], BF16, name="x")
+                nc.sync.dma_start(out=x_half[(b, g)][:], in_=halves[g])
+
+        for b in range(BATCH - 1):
+            load(b)
 
         ident = const.tile([P, P], F32)
         make_identity(nc, ident[:])
@@ -170,6 +173,8 @@ def tile_reasoningmultiheadattention_pb_t_kernel(tc, h_attn, Wo, bo, out):
         first_multiply = QUADS + len(block_stages)
         steps_per_product = N_BLOCKS // N_PRODUCTS
         for step in range(first_multiply + steps_per_product * (N_PRODUCTS - 1) + 2):
+            if step == BLOCKS_PER_BATCH:
+                load(BATCH - 1)
             for lag, stage in enumerate(block_stages):
                 if 0 <= step - lag < N_BLOCKS:
                     stage(step - lag)

@@ -97,7 +97,9 @@ def tile_reasoningmultiheadattention_pb_t_kernel(tc, h_attn, Wo, bo, out):
             mine = slice(quad * QUAD, (quad + 1) * QUAD)
             heads = heads_pool.tile([P, QUAD, PLANES, J_PER_PASS, WORDS // PLANES], F32)
             words = x[:].bitcast(F32)[:, :, mine, :].rearrange("p j h (w u) -> p h u j w", u=PLANES)
-            if b > 0 and (block % BLOCKS_PER_BATCH) % 3 == 1:
+            if b > 0 and block % 2 == 1:
+                nc.gpsimd.tensor_copy(out=heads[:], in_=words)
+            elif b > 0 and block % 4 == 2:
                 nc.scalar.copy(out=heads[:], in_=words)
             else:
                 nc.vector.tensor_copy(out=heads[:], in_=words)
@@ -167,7 +169,11 @@ def tile_reasoningmultiheadattention_pb_t_kernel(tc, h_attn, Wo, bo, out):
                     in1=bias[:],
                     op=mybir.AluOpType.add,
                 )
-            nc.sync.dma_start(out=slabs[quad], in_=res[:])
+                if product == N_PRODUCTS - 1:
+                    rows = slice(half * PER_BANK, (half + 1) * PER_BANK)
+                    nc.sync.dma_start(out=slabs[quad][:, rows], in_=res[:, rows])
+            if product < N_PRODUCTS - 1:
+                nc.sync.dma_start(out=slabs[quad], in_=res[:])
 
         block_stages = [regroup, transpose, interleave, quantise]
         first_multiply = QUADS + len(block_stages)

@@ -39,7 +39,7 @@ def tile_reasoningmultiheadattention_pb_t_kernel(tc, h_attn, Wo, bo, out):
         heads_pool = ctx.enter_context(tc.tile_pool(name="heads", bufs=5))
         grouped_pool = ctx.enter_context(tc.tile_pool(name="grouped", bufs=5))
         codes_pool = ctx.enter_context(tc.tile_pool(name="codes", bufs=2 * QUADS + 1))
-        res_pool = ctx.enter_context(tc.tile_pool(name="res", bufs=14))
+        res_pool = ctx.enter_context(tc.tile_pool(name="res", bufs=1))
         psum_t = ctx.enter_context(tc.psum_pool(name="psum_t", bufs=4))
         psum_o = ctx.enter_context(tc.psum_pool(name="psum_o", bufs=4))
         ctx.enter_context(tc.manual_schedule())
@@ -89,7 +89,7 @@ def tile_reasoningmultiheadattention_pb_t_kernel(tc, h_attn, Wo, bo, out):
         def where(block):
             return block // BLOCKS_PER_BATCH, (block // QUADS) % PASSES, block % QUADS
 
-        heads_of, banks_of, grouped_of, codes_of, scales_of, acc_of = {}, {}, {}, {}, {}, {}
+        heads_of, banks_of, grouped_of, codes_of, scales_of, acc_of, res_of = {}, {}, {}, {}, {}, {}, {}
 
         def regroup(block):
             b, g, quad = where(block)
@@ -160,20 +160,32 @@ def tile_reasoningmultiheadattention_pb_t_kernel(tc, h_attn, Wo, bo, out):
 
         def add_bias_and_store(product):
             b, quad = product // QUADS, product % QUADS
-            slabs = out[b].rearrange("(s m c) n -> s m c n", m=P, c=QUAD)
-            res = res_pool.tile([P, QUAD, HID], F32)
+            together = product < N_PRODUCTS // 2
+            if together:
+                i = quad % 2
+                if i == 0:
+                    res_of[product // 2] = res_pool.tile([P, 2, QUAD, HID], F32, name="res_two", bufs=4)
+                res = res_of[product // 2][:, i]
+            else:
+                res = res_pool.tile([P, QUAD, HID], F32, name="res", bufs=6)[:]
+            slabs = out[b].rearrange("(s m c) n -> m s (c n)", m=P, c=QUAD)
             for half, acc in enumerate(acc_of[product]):
+                rows = slice(half * PER_BANK, (half + 1) * PER_BANK)
                 nc.vector.tensor_tensor(
-                    out=res[:, half * PER_BANK : (half + 1) * PER_BANK, :],
-                    in0=acc[:],
-                    in1=bias[:],
-                    op=mybir.AluOpType.add,
+                    out=res[:, rows, :], in0=acc[:], in1=bias[:], op=mybir.AluOpType.add
                 )
                 if product == N_PRODUCTS - 1:
-                    rows = slice(half * PER_BANK, (half + 1) * PER_BANK)
-                    nc.sync.dma_start(out=slabs[quad][:, rows], in_=res[:, rows])
-            if product < N_PRODUCTS - 1:
-                nc.sync.dma_start(out=slabs[quad], in_=res[:])
+                    cols = slice(half * PER_BANK * HID, (half + 1) * PER_BANK * HID)
+                    nc.sync.dma_start(
+                        out=slabs[:, quad, cols], in_=res[:, rows, :].rearrange("p c n -> p (c n)")
+                    )
+            if together and quad % 2 == 1:
+                nc.sync.dma_start(
+                    out=slabs[:, quad - 1 : quad + 1, :],
+                    in_=res_of[product // 2][:].rearrange("p i c n -> p i (c n)"),
+                )
+            elif not together and product < N_PRODUCTS - 1:
+                nc.sync.dma_start(out=slabs[:, quad, :], in_=res.rearrange("p c n -> p (c n)"))
 
         block_stages = [regroup, transpose, interleave, quantise]
         first_multiply = QUADS + len(block_stages)

from contextlib import ExitStack

import concourse.mybir as mybir
from concourse.masks import make_identity

BF16 = mybir.dt.bfloat16
F32 = mybir.dt.float32
U32 = mybir.dt.uint32
U8 = mybir.dt.uint8
FP8X4 = mybir.dt.float8_e4m3fn_x4

P = 128
BATCH = 4
TOKENS = 2048
HEADS = 16
DH = 64
HID = 256
TOKENS_PER_ROW = 16
PASSES = 2
J_PER_PASS = TOKENS_PER_ROW // PASSES
PLANES = 2
WORDS = DH // 2
QUAD = 4
QUADS = HEADS // QUAD
PER_BANK = 2
BANKS = QUAD // PER_BANK
BLOCKS_PER_BATCH = PASSES * QUADS
N_BLOCKS = BATCH * BLOCKS_PER_BATCH
N_PRODUCTS = BATCH * QUADS

FLOPS = 2 * BATCH * TOKENS * (TOKENS_PER_ROW * DH) * HID


def tile_reasoningmultiheadattention_pb_t_kernel(tc, h_attn, Wo, bo, out):
    nc = tc.nc
    with ExitStack() as ctx:
        const = ctx.enter_context(tc.tile_pool(name="const", bufs=1))
        x_pool = ctx.enter_context(tc.tile_pool(name="x", bufs=6))
        heads_pool = ctx.enter_context(tc.tile_pool(name="heads", bufs=5))
        grouped_pool = ctx.enter_context(tc.tile_pool(name="grouped", bufs=5))
        codes_pool = ctx.enter_context(tc.tile_pool(name="codes", bufs=2 * QUADS + 1))
        res_pool = ctx.enter_context(tc.tile_pool(name="res", bufs=1))
        psum_t = ctx.enter_context(tc.psum_pool(name="psum_t", bufs=4))
        psum_o = ctx.enter_context(tc.psum_pool(name="psum_o", bufs=4))
        ctx.enter_context(tc.manual_schedule())

        w_raw = const.tile([P, PASSES, 2 * PLANES, HID], BF16)
        nc.sync.dma_start(
            out=w_raw[:].rearrange("p g t n -> p g (t n)"),
            in_=Wo.rearrange("(g p t) n -> p g (t n)", p=P, t=2 * PLANES),
        )
        bias_row = const.tile([P, HID], BF16)
        nc.vector.memset(bias_row[:], 0.0)
        nc.sync.dma_start(out=bias_row[0:1, :], in_=bo.rearrange("(o n) -> o n", o=1))
        x_half = {}

        def load(b):
            halves = h_attn[b].rearrange("(r g j) h d -> g r j h d", g=PASSES, j=J_PER_PASS)
            for g in range(PASSES):
                x_half[(b, g)] = x_pool.tile([P, J_PER_PASS, HEADS, DH], BF16, name="x")
                nc.sync.dma_start(out=x_half[(b, g)][:], in_=halves[g])

        for b in range(BATCH - 1):
            load(b)

        ident = const.tile([P, P], F32)
        make_identity(nc, ident[:])
        ones = const.tile([P, P], BF16)
        nc.vector.memset(ones[:], 1.0)

        w_grouped = const.tile([P, PASSES, HID, 2 * PLANES], BF16, align_bytes=64)
        nc.vector.tensor_copy(out=w_grouped[:], in_=w_raw[:].rearrange("p g t n -> p g n t"))
        w_codes = const.tile([P, PASSES * HID], U32, align_bytes=64)
        w_scales = const.tile([P, PASSES * HID], U8, align_bytes=64)
        nc.vector.quantize_mx(
            out=w_codes[:].bitcast(FP8X4),
            scales=w_scales[:],
            in_=w_grouped[:].rearrange("p g n t -> p (g n t)"),
        )

        bias_ps = psum_o.tile([P, PER_BANK, HID], F32, tag="acc")
        for c in range(PER_BANK):
            nc.tensor.matmul(
                out=bias_ps[:, c, :], lhsT=ones[:], rhs=bias_row[:], start=True, stop=True
            )
        bias = const.tile([P, PER_BANK, HID], F32)
        nc.scalar.copy(out=bias[:], in_=bias_ps[:])

        def where(block):
            return block // BLOCKS_PER_BATCH, (block // QUADS) % PASSES, block % QUADS

        heads_of, banks_of, grouped_of, codes_of, scales_of, acc_of, res_of = {}, {}, {}, {}, {}, {}, {}

        def regroup(block):
            b, g, quad = where(block)
            x = x_half[(b, g)]
            mine = slice(quad * QUAD, (quad + 1) * QUAD)
            heads = heads_pool.tile([P, QUAD, PLANES, J_PER_PASS, WORDS // PLANES], F32)
            words = x[:].bitcast(F32)[:, :, mine, :].rearrange("p j h (w u) -> p h u j w", u=PLANES)
            if b > 0 and block % 2 == 1:
                nc.gpsimd.tensor_copy(out=heads[:], in_=words)
            elif b > 0 and block % 4 == 2:
                nc.scalar.copy(out=heads[:], in_=words)
            else:
                nc.vector.tensor_copy(out=heads[:], in_=words)
            heads_of[block] = heads

        def transpose(block):
            words = heads_of[block][:].rearrange("p h u j w -> p h u (j w)")
            banks_of[block] = []
            for half in range(BANKS):
                bank = psum_t.tile([P, PLANES, PER_BANK * P], F32)
                for h in range(PER_BANK):
                    for u in range(PLANES):
                        nc.tensor.transpose(
                            bank[:, u, h * P : (h + 1) * P], words[:, half * PER_BANK + h, u, :], ident[:]
                        )
                banks_of[block].append(bank)

        def interleave(block):
            grouped = grouped_pool.tile([P, QUAD, P, 2 * PLANES], BF16, align_bytes=64)
            words = grouped[:].bitcast(F32)
            for half, bank in enumerate(banks_of[block]):
                nc.scalar.copy(
                    out=words[:, :, half * P // BANKS : (half + 1) * P // BANKS, :],
                    in_=bank[:].rearrange("p u (m c) -> p c m u", c=QUAD),
                )
            grouped_of[block] = grouped

        def quantise(block):
            codes = codes_pool.tile([P, QUAD * P], U32, align_bytes=64)
            scales = codes_pool.tile([P, QUAD * P], U8, align_bytes=64)
            nc.vector.quantize_mx(
                out=codes[:].bitcast(FP8X4),
                scales=scales[:],
                in_=grouped_of[block][:].rearrange("p c m t -> p (c m t)"),
            )
            codes_of[block], scales_of[block] = codes, scales

        def multiply(product):
            b, quad = product // QUADS, product % QUADS
            block_of_pass = [b * BLOCKS_PER_BATCH + g * QUADS + quad for g in range(PASSES)]
            acc_of[product] = []
            for half in range(BANKS):
                acc = psum_o.tile([P, PER_BANK, HID], F32, tag="acc")
                for c in range(PER_BANK):
                    row_tile = slice((half * PER_BANK + c) * P, (half * PER_BANK + c + 1) * P)
                    for g in range(PASSES):
                        n_cols = slice(g * HID, (g + 1) * HID)
                        nc.tensor.matmul_mx(
                            out=acc[:, c, :],
                            lhsT=codes_of[block_of_pass[g]][:, row_tile].bitcast(FP8X4),
                            lhsT_scale=scales_of[block_of_pass[g]][:, row_tile],
                            rhs=w_codes[:, n_cols].bitcast(FP8X4),
                            rhs_scale=w_scales[:, n_cols],
                            start=(g == 0),
                            stop=(g == PASSES - 1),
                        )
                acc_of[product].append(acc)

        def add_bias_and_store(product):
            b, quad = product // QUADS, product % QUADS
            together = product < N_PRODUCTS // 2
            if together:
                i = quad % 2
                if i == 0:
                    res_of[product // 2] = res_pool.tile([P, 2, QUAD, HID], F32, name="res_two", bufs=4)
                res = res_of[product // 2][:, i]
            else:
                res = res_pool.tile([P, QUAD, HID], F32, name="res", bufs=6)[:]
            slabs = out[b].rearrange("(s m c) n -> m s (c n)", m=P, c=QUAD)
            for half, acc in enumerate(acc_of[product]):
                rows = slice(half * PER_BANK, (half + 1) * PER_BANK)
                nc.vector.tensor_tensor(
                    out=res[:, rows, :], in0=acc[:], in1=bias[:], op=mybir.AluOpType.add
                )
                if product == N_PRODUCTS - 1:
                    cols = slice(half * PER_BANK * HID, (half + 1) * PER_BANK * HID)
                    nc.sync.dma_start(
                        out=slabs[:, quad, cols], in_=res[:, rows, :].rearrange("p c n -> p (c n)")
                    )
            if together and quad % 2 == 1:
                nc.sync.dma_start(
                    out=slabs[:, quad - 1 : quad + 1, :],
                    in_=res_of[product // 2][:].rearrange("p i c n -> p i (c n)"),
                )
            elif not together and product < N_PRODUCTS - 1:
                nc.sync.dma_start(out=slabs[:, quad, :], in_=res.rearrange("p c n -> p (c n)"))

        block_stages = [regroup, transpose, interleave, quantise]
        first_multiply = QUADS + len(block_stages)
        steps_per_product = N_BLOCKS // N_PRODUCTS
        for step in range(first_multiply + steps_per_product * (N_PRODUCTS - 1) + 2):
            if step == BLOCKS_PER_BATCH:
                load(BATCH - 1)
            for lag, stage in enumerate(block_stages):
                if 0 <= step - lag < N_BLOCKS:
                    stage(step - lag)
            for lag, stage in enumerate([multiply, add_bias_and_store], start=first_multiply):
                if step >= lag and (step - lag) % steps_per_product == 0:
                    if (step - lag) // steps_per_product < N_PRODUCTS:
                        stage((step - lag) // steps_per_product)
